import numpy as np
import ml_dtypes


def mxq(x, axis, fmt="e4m3"):
    dtype, down = {"e4m3": (ml_dtypes.float8_e4m3fn, 7), "e5m2": (ml_dtypes.float8_e5m2, 14)}[fmt]
    v = np.moveaxis(np.asarray(x, np.float32).astype(ml_dtypes.bfloat16).astype(np.float64), axis, -1)
    blocks = v.reshape(v.shape[:-1] + (-1, 32))
    amax = np.abs(blocks).max(-1, keepdims=True)
    byte = np.maximum(np.where(amax > 0, np.frexp(amax)[1] - 1 + 127, 0) - down, 1)
    scale = np.exp2(byte - 127.0)
    codes = (blocks / scale).astype(np.float32).astype(dtype).astype(np.float64)
    return np.moveaxis((codes * scale).reshape(v.shape), -1, axis)


WIDE = False


def mx_kscale(k):
    if not WIDE:
        return np.ones(k)
    levels = np.array([10, -10, 5, -5, 0])
    a = np.random.permutation(np.resize(levels, k // 512 * 4)).reshape(k // 512, 4)
    idx = np.arange(k)
    return np.exp2(a[idx // 512, idx % 128 // 32])


BF16 = ml_dtypes.bfloat16


def bf(x):
    return np.asarray(x, np.float32).astype(BF16)


def f64(x):
    return np.asarray(x).astype(np.float64)


E2M1 = np.array([0.0, 0.5, 1.0, 1.5, 2.0, 3.0, 4.0, 6.0, -0.0, -0.5, -1.0, -1.5, -2.0, -3.0, -4.0, -6.0])


def pack_weight(w, fmt):
    k, n = w.shape
    w = f64(bf(w)).reshape(k // 32, 32, n)
    amax = np.abs(w).max(1)
    if fmt == "e4m3":
        byte = np.frexp(amax)[1] - 1 + 127 - 7
    else:
        mant, ex = np.frexp(amax / 6.0)
        byte = np.where(mant > 0.5, ex, ex - 1) + 127
    byte = np.clip(np.where(amax > 0, byte, 1), 1, 254)
    scaled = (w * np.exp2(127.0 - byte)[:, None, :]).reshape(k, n).astype(np.float32)
    by_word = np.ascontiguousarray(scaled.reshape(k // 512, 128, 4, n).transpose(0, 1, 3, 2))
    if fmt == "e4m3":
        words = by_word.astype(ml_dtypes.float8_e4m3fn).view(np.uint8)
    else:
        c = by_word.astype(ml_dtypes.float4_e2m1fn).view(np.uint8) & 0xF
        words = c[..., 0::2] | (c[..., 1::2] << 4)
    return np.ascontiguousarray(words), np.ascontiguousarray(byte.astype(np.uint8).reshape(k // 512, 16, n))


def unpack_weight(words, scales, fmt):
    g, p, n, _ = words.shape
    if fmt == "e4m3":
        vals = np.ascontiguousarray(words).view(ml_dtypes.float8_e4m3fn).astype(np.float64)
    else:
        nib = np.empty((g, p, n, 4), np.uint8)
        nib[..., 0::2] = words & 0xF
        nib[..., 1::2] = words >> 4
        vals = E2M1[nib]
    vals = vals * np.repeat(np.exp2(scales.astype(np.float64) - 127.0), 8, axis=1)[..., None]
    return vals.transpose(0, 1, 3, 2).reshape(g * 512, n)


B, T, S, St, H = 4, 128, 1024, 512, 1024
K3 = 3 * H
H2 = 2 * H
FMT = "e4m3"


def sigmoid(v):
    return 1.0 / (1.0 + np.exp(-v))


def setup_inputs():
    s = mx_kscale(K3)
    k_s, k_t, k_o = s[:H], s[H:H2], s[H2:]
    sent_ctx = bf(np.random.standard_normal((B, T, H)) * 0.25 * k_s)
    template_ctx = bf(np.random.standard_normal((B, T, H)) * 0.25 * k_t)
    output = bf(np.random.standard_normal((B, T, H)) * 0.2 * k_o)
    w_gate = np.random.standard_normal((H, K3)) * 6.0 / np.sqrt(K3) / s[None, :]
    w_sent = np.random.standard_normal((H, H)) * 3.0 / np.sqrt(H) / k_s[None, :]
    w_template = np.random.standard_normal((H, H)) * 3.0 / np.sqrt(H) / k_t[None, :]
    w_output = np.random.standard_normal((H, H)) * 3.0 / np.sqrt(H) / k_o[None, :]
    gate_words, gate_scales = pack_weight(np.ascontiguousarray(w_gate.T), FMT)
    sent_words, sent_scales = pack_weight(np.ascontiguousarray(w_sent.T), FMT)
    template_words, template_scales = pack_weight(np.ascontiguousarray(w_template.T), FMT)
    output_words, output_scales = pack_weight(np.ascontiguousarray(w_output.T), FMT)
    return {
        "sent_ctx": sent_ctx,
        "template_ctx": template_ctx,
        "output": output,
        "W_gate_words": gate_words,
        "W_gate_scales": gate_scales,
        "W_sent_words": sent_words,
        "W_sent_scales": sent_scales,
        "W_template_words": template_words,
        "W_template_scales": template_scales,
        "W_output_words": output_words,
        "W_output_scales": output_scales,
    }


def reference(sent_ctx, template_ctx, output, W_gate_words, W_gate_scales, W_sent_words, W_sent_scales,
              W_template_words, W_template_scales, W_output_words, W_output_scales):
    cat = np.concatenate([f64(sent_ctx), f64(template_ctx), f64(output)], axis=-1)
    catq = mxq(cat, 2, "e4m3")
    sq, tq, oq = catq[..., :H], catq[..., H:H2], catq[..., H2:]
    gate = sigmoid(catq @ unpack_weight(W_gate_words, W_gate_scales, FMT))
    fusion = ((1.0 - gate) * (sq @ unpack_weight(W_sent_words, W_sent_scales, FMT))
              + gate * (tq @ unpack_weight(W_template_words, W_template_scales, FMT))
              + (oq @ unpack_weight(W_output_words, W_output_scales, FMT)))
    return np.tanh(fusion)

@@ -1,0 +1,211 @@
+from contextlib import ExitStack
+
+import concourse.mybir as mybir
+from concourse.masks import make_identity
+
+BF16 = mybir.dt.bfloat16
+F32 = mybir.dt.float32
+I32 = mybir.dt.int32
+U32 = mybir.dt.uint32
+U8 = mybir.dt.uint8
+FP8X4 = mybir.dt.float8_e4m3fn_x4
+ACT = mybir.ActivationFunctionType
+ALU = mybir.AluOpType
+
+P = 128
+PACK = 4
+K_PASS = P * PACK
+PAIRS = K_PASS // 2
+H = 1024
+TOKENS = 512
+TOKEN_TILES = TOKENS // P
+SOURCES = 3
+GROUPS = H // K_PASS
+N_PASS = 512
+HALVES = H // N_PASS
+GATE_SLOTS = SOURCES * GROUPS
+SLOTS = 2 * GATE_SLOTS
+PLANES_PER_TILE = 4
+QUADRANTS = 4
+LIVE_ROWS = 4
+
+FLOPS = 2 * TOKENS * H * (SOURCES * H + SOURCES * H)
+
+
+def tile_attention_two_encoder_pa_kernel(
+    tc,
+    sent_ctx,
+    template_ctx,
+    output,
+    W_gate_words,
+    W_gate_scales,
+    W_sent_words,
+    W_sent_scales,
+    W_template_words,
+    W_template_scales,
+    W_output_words,
+    W_output_scales,
+    out,
+):
+    nc = tc.nc
+    sources = [sent_ctx, template_ctx, output]
+
+    def by_partition(tensor):
+        return tensor.rearrange("b t c -> (b t) c").rearrange("(p j) c -> p j c", j=TOKEN_TILES)
+
+    out_rows = by_partition(out)
+
+    with ExitStack() as stack:
+        keep = stack.enter_context(tc.tile_pool(name="keep", bufs=1))
+        work = stack.enter_context(tc.tile_pool(name="work", bufs=4))
+        psum = stack.enter_context(tc.psum_pool(name="psum", bufs=8))
+        stack.enter_context(tc.manual_schedule())
+
+        x_rows = [keep.tile([P, TOKEN_TILES, H], BF16, name="x_rows%d" % s) for s in range(SOURCES)]
+        x_grouped = [
+            keep.tile([P, TOKEN_TILES, GROUPS, P, PACK], BF16, name="x_grouped%d" % s, align_bytes=64)
+            for s in range(SOURCES)
+        ]
+        x_codes = keep.tile([P, SOURCES, TOKEN_TILES, GROUPS, P], U32, align_bytes=64)
+        x_planes = keep.tile([P, SOURCES, TOKEN_TILES, GROUPS, P], U8, align_bytes=64)
+        w_codes = keep.tile([P, SLOTS, H], U32, align_bytes=64)
+        w_planes = keep.tile([P, SLOTS // PLANES_PER_TILE, H], U8, align_bytes=64)
+        identity = keep.tile([P, P], F32)
+        warm = keep.tile([P, 1], F32)
+
+        nc.vector.memset(w_planes[:].bitcast(I32), 0)
+        nc.vector.memset(warm[:], 0.0)
+        nc.scalar.activation(out=warm[:], in_=warm[:], func=ACT.Sigmoid)
+        make_identity(nc, identity[:])
+
+        def load_source(s):
+            nc.sync.dma_start(out=x_rows[s][:], in_=by_partition(sources[s]))
+
+        def columns(half):
+            return slice(half * N_PASS, (half + 1) * N_PASS)
+
+        def load_codes(words, first, count, slot, half):
+            byte_columns = slice(half * N_PASS * PACK, (half + 1) * N_PASS * PACK)
+            nc.sync.dma_start(
+                out=w_codes[:, slot : slot + count, columns(half)].bitcast(I32),
+                in_=words[first : first + count]
+                .rearrange("g p n t -> p g (n t)")[:, :, byte_columns]
+                .bitcast(I32),
+            )
+
+        def plane_rows(slot):
+            return LIVE_ROWS * (slot % PLANES_PER_TILE)
+
+        def load_scales(scales, first, count, slot):
+            for quadrant in range(QUADRANTS):
+                top = 32 * quadrant + plane_rows(slot)
+                nc.sync.dma_start(
+                    out=w_planes[top : top + LIVE_ROWS * count, slot // PLANES_PER_TILE, :].bitcast(I32),
+                    in_=scales[
+                        first : first + count, LIVE_ROWS * quadrant : LIVE_ROWS * (quadrant + 1), :
+                    ].bitcast(I32),
+                )
+
+        projections = [
+            (W_sent_words, W_sent_scales),
+            (W_template_words, W_template_scales),
+            (W_output_words, W_output_scales),
+        ]
+
+        load_source(0)
+        load_scales(W_gate_scales, 0, 4, 0)
+        load_source(1)
+        load_source(2)
+        load_codes(W_gate_words, 0, GROUPS, 0, 0)
+        load_scales(W_gate_scales, 4, 2, 4)
+        load_codes(W_gate_words, 2, GROUPS, 2, 0)
+        load_codes(W_gate_words, 4, GROUPS, 4, 0)
+        for s, (words, scales) in enumerate(projections):
+            load_scales(scales, 0, GROUPS, GATE_SLOTS + GROUPS * s)
+        for s, (words, scales) in enumerate(projections):
+            load_codes(words, 0, GROUPS, GATE_SLOTS + GROUPS * s, 0)
+        for s in range(SOURCES):
+            load_codes(W_gate_words, GROUPS * s, GROUPS, GROUPS * s, 1)
+        for s, (words, scales) in enumerate(projections):
+            load_codes(words, 0, GROUPS, GATE_SLOTS + GROUPS * s, 1)
+
+        def quantise(s, j):
+            nc.vector.quantize_mx(
+                out=x_codes[:, s, j].rearrange("p g r -> p (g r)").bitcast(FP8X4),
+                scales=x_planes[:, s, j].rearrange("p g r -> p (g r)"),
+                in_=x_grouped[s][:, j].rearrange("p g r t -> p (g r t)"),
+            )
+
+        for s in range(SOURCES):
+            for j in range(TOKEN_TILES):
+                pairs = x_rows[s][:, j, :].bitcast(F32)
+                flipped = psum.tile([P, GROUPS, 2, P], F32, tag="bank")
+                for g in range(GROUPS):
+                    for u in range(2):
+                        nc.tensor.transpose(
+                            flipped[:, g, u, :],
+                            pairs[:, PAIRS * g + u : PAIRS * (g + 1) : 2],
+                            identity[:],
+                        )
+                copy = nc.vector.tensor_copy if j == TOKEN_TILES - 1 else nc.scalar.copy
+                copy(
+                    out=x_grouped[s][:, j].bitcast(F32),
+                    in_=flipped[:].rearrange("p g u r -> p g r u"),
+                )
+                if j > 0:
+                    quantise(s, j - 1)
+            quantise(s, TOKEN_TILES - 1)
+
+        def product(chain, half, tiles):
+            banks = {}
+            for j in tiles:
+                banks[j] = psum.tile([P, N_PASS], F32, name="bank%d" % j, tag="bank")
+            for step, (s, g, slot) in enumerate(chain):
+                for j in tiles:
+                    nc.tensor.matmul_mx(
+                        out=banks[j][:],
+                        lhsT=x_codes[:, s, j, g, :].bitcast(FP8X4),
+                        lhsT_scale=x_planes[:, s, j, g, :],
+                        rhs=w_codes[:, slot, columns(half)].bitcast(FP8X4),
+                        rhs_scale=w_planes[plane_rows(slot) : P, slot // PLANES_PER_TILE, columns(half)],
+                        start=(step == 0),
+                        stop=(step == len(chain) - 1),
+                    )
+            return banks
+
+        def projection_chain(s):
+            return [(s, g, GATE_SLOTS + GROUPS * s + g) for g in range(GROUPS)]
+
+        gate_chain = [(s, g, GROUPS * s + g) for s in range(SOURCES) for g in range(GROUPS)]
+        gates = {}
+
+        def gate_round(half, tiles):
+            banks = product(gate_chain, half, tiles)
+            for j in tiles:
+                gates[j] = work.tile([P, N_PASS], F32, name="gate%d" % j, tag="gate", bufs=6)
+                nc.scalar.activation(out=gates[j][:], in_=banks[j][:], func=ACT.Sigmoid)
+
+        def fusion_round(half, j):
+            from_sent = product(projection_chain(0), half, [j])[j]
+            kept = work.tile([P, N_PASS], F32)
+            nc.vector.scalar_tensor_tensor(
+                out=kept[:], in0=gates[j][:], scalar=1.0, in1=from_sent[:], op0=ALU.subtract, op1=ALU.mult
+            )
+            from_template = product(projection_chain(1), half, [j])[j]
+            taken = work.tile([P, N_PASS], F32)
+            nc.vector.tensor_tensor(out=taken[:], in0=gates[j][:], in1=from_template[:], op=ALU.mult)
+            mixed = work.tile([P, N_PASS], F32)
+            nc.vector.tensor_tensor(out=mixed[:], in0=taken[:], in1=kept[:], op=ALU.subtract)
+            from_output = product(projection_chain(2), half, [j])[j]
+            fusion = work.tile([P, N_PASS], F32)
+            nc.vector.tensor_tensor(out=fusion[:], in0=mixed[:], in1=from_output[:], op=ALU.add)
+            result = work.tile([P, N_PASS], F32, bufs=8)
+            nc.scalar.activation(out=result[:], in_=fusion[:], func=ACT.Tanh)
+            nc.sync.dma_start(out=out_rows[:, j, columns(half)], in_=result[:])
+
+        gate_round(0, range(TOKEN_TILES))
+        for j in range(TOKEN_TILES):
+            fusion_round(0, j)
+        for j in range(TOKEN_TILES):
+            gate_round(1, [j])
+            fusion_round(1, j)

@@ -185,7 +185,9 @@ def tile_attention_two_encoder_pa_kernel(
                 gates[j] = work.tile([P, N_PASS], F32, name="gate%d" % j, tag="gate", bufs=6)
                 nc.scalar.activation(out=gates[j][:], in_=banks[j][:], func=ACT.Sigmoid)
 
-        def fusion_round(half, j):
+        mixes = {}
+
+        def blend(half, j):
             from_sent = product(projection_chain(0), half, [j])[j]
             kept = work.tile([P, N_PASS], F32)
             nc.vector.scalar_tensor_tensor(
@@ -194,18 +196,23 @@ def tile_attention_two_encoder_pa_kernel(
             from_template = product(projection_chain(1), half, [j])[j]
             taken = work.tile([P, N_PASS], F32)
             nc.vector.tensor_tensor(out=taken[:], in0=gates[j][:], in1=from_template[:], op=ALU.mult)
-            mixed = work.tile([P, N_PASS], F32)
-            nc.vector.tensor_tensor(out=mixed[:], in0=taken[:], in1=kept[:], op=ALU.subtract)
+            mixes[j] = work.tile([P, N_PASS], F32, name="mixed")
+            nc.gpsimd.tensor_tensor(out=mixes[j][:], in0=taken[:], in1=kept[:], op=ALU.subtract)
+
+        def finish(half, j):
             from_output = product(projection_chain(2), half, [j])[j]
             fusion = work.tile([P, N_PASS], F32)
-            nc.vector.tensor_tensor(out=fusion[:], in0=mixed[:], in1=from_output[:], op=ALU.add)
+            nc.vector.tensor_tensor(out=fusion[:], in0=mixes[j][:], in1=from_output[:], op=ALU.add)
             result = work.tile([P, N_PASS], F32, bufs=8)
             nc.scalar.activation(out=result[:], in_=fusion[:], func=ACT.Tanh)
             nc.sync.dma_start(out=out_rows[:, j, columns(half)], in_=result[:])
 
+        units = [(half, j) for half in range(HALVES) for j in range(TOKEN_TILES)]
         gate_round(0, range(TOKEN_TILES))
-        for j in range(TOKEN_TILES):
-            fusion_round(0, j)
-        for j in range(TOKEN_TILES):
-            gate_round(1, [j])
-            fusion_round(1, j)
+        for before, (half, j), after in zip([None] + units, units, units[1:] + [None]):
+            blend(half, j)
+            if after is not None and after[0] > 0:
+                gate_round(after[0], [after[1]])
+            if before is not None:
+                finish(before[0], before[1])
+        finish(HALVES - 1, TOKEN_TILES - 1)

@@ -22,7 +22,9 @@ TOKEN_TILES = TOKENS // P
 SOURCES = 3
 GROUPS = H // K_PASS
 N_PASS = 512
-HALVES = H // N_PASS
+HALVES = [(0, N_PASS), (N_PASS, N_PASS)]
+BLOCKS = [(0, N_PASS), (N_PASS, N_PASS // 2), (N_PASS + N_PASS // 2, N_PASS // 2)]
+TILES_PER_LOAD = 2
 GATE_SLOTS = SOURCES * GROUPS
 SLOTS = 2 * GATE_SLOTS
 PLANES_PER_TILE = 4
@@ -61,7 +63,10 @@ def tile_attention_two_encoder_pa_kernel(
         psum = stack.enter_context(tc.psum_pool(name="psum", bufs=8))
         stack.enter_context(tc.manual_schedule())
 
-        x_rows = [keep.tile([P, TOKEN_TILES, H], BF16, name="x_rows%d" % s) for s in range(SOURCES)]
+        x_rows = {}
+        for s in range(SOURCES):
+            for j in range(0, TOKEN_TILES, TILES_PER_LOAD):
+                x_rows[s, j] = keep.tile([P, TILES_PER_LOAD, H], BF16, name="x_rows%d_%d" % (s, j))
         x_grouped = [
             keep.tile([P, TOKEN_TILES, GROUPS, P, PACK], BF16, name="x_grouped%d" % s, align_bytes=64)
             for s in range(SOURCES)
@@ -79,13 +84,14 @@ def tile_attention_two_encoder_pa_kernel(
         make_identity(nc, identity[:])
 
         def load_source(s):
-            nc.sync.dma_start(out=x_rows[s][:], in_=by_partition(sources[s]))
+            for j in range(0, TOKEN_TILES, TILES_PER_LOAD):
+                nc.sync.dma_start(out=x_rows[s, j][:], in_=by_partition(sources[s])[:, j : j + TILES_PER_LOAD, :])
 
-        def columns(half):
-            return slice(half * N_PASS, (half + 1) * N_PASS)
+        def columns(block):
+            return slice(block[0], block[0] + block[1])
 
         def load_codes(words, first, count, slot, half):
-            byte_columns = slice(half * N_PASS * PACK, (half + 1) * N_PASS * PACK)
+            byte_columns = slice(half[0] * PACK, (half[0] + half[1]) * PACK)
             nc.sync.dma_start(
                 out=w_codes[:, slot : slot + count, columns(half)].bitcast(I32),
                 in_=words[first : first + count]
@@ -116,18 +122,18 @@ def tile_attention_two_encoder_pa_kernel(
         load_scales(W_gate_scales, 0, 4, 0)
         load_source(1)
         load_source(2)
-        load_codes(W_gate_words, 0, GROUPS, 0, 0)
+        load_codes(W_gate_words, 0, GROUPS, 0, HALVES[0])
         load_scales(W_gate_scales, 4, 2, 4)
-        load_codes(W_gate_words, 2, GROUPS, 2, 0)
-        load_codes(W_gate_words, 4, GROUPS, 4, 0)
+        load_codes(W_gate_words, 2, GROUPS, 2, HALVES[0])
+        load_codes(W_gate_words, 4, GROUPS, 4, HALVES[0])
         for s, (words, scales) in enumerate(projections):
             load_scales(scales, 0, GROUPS, GATE_SLOTS + GROUPS * s)
         for s, (words, scales) in enumerate(projections):
-            load_codes(words, 0, GROUPS, GATE_SLOTS + GROUPS * s, 0)
+            load_codes(words, 0, GROUPS, GATE_SLOTS + GROUPS * s, HALVES[0])
         for s in range(SOURCES):
-            load_codes(W_gate_words, GROUPS * s, GROUPS, GROUPS * s, 1)
+            load_codes(W_gate_words, GROUPS * s, GROUPS, GROUPS * s, HALVES[1])
         for s, (words, scales) in enumerate(projections):
-            load_codes(words, 0, GROUPS, GATE_SLOTS + GROUPS * s, 1)
+            load_codes(words, 0, GROUPS, GATE_SLOTS + GROUPS * s, HALVES[1])
 
         def quantise(s, j):
             nc.vector.quantize_mx(
@@ -138,7 +144,7 @@ def tile_attention_two_encoder_pa_kernel(
 
         for s in range(SOURCES):
             for j in range(TOKEN_TILES):
-                pairs = x_rows[s][:, j, :].bitcast(F32)
+                pairs = x_rows[s, j - j % TILES_PER_LOAD][:, j % TILES_PER_LOAD, :].bitcast(F32)
                 flipped = psum.tile([P, GROUPS, 2, P], F32, tag="bank")
                 for g in range(GROUPS):
                     for u in range(2):
@@ -156,18 +162,18 @@ def tile_attention_two_encoder_pa_kernel(
                     quantise(s, j - 1)
             quantise(s, TOKEN_TILES - 1)
 
-        def product(chain, half, tiles):
+        def product(chain, block, tiles):
             banks = {}
             for j in tiles:
-                banks[j] = psum.tile([P, N_PASS], F32, name="bank%d" % j, tag="bank")
+                banks[j] = psum.tile([P, block[1]], F32, name="bank%d" % j, tag="bank")
             for step, (s, g, slot) in enumerate(chain):
                 for j in tiles:
                     nc.tensor.matmul_mx(
                         out=banks[j][:],
                         lhsT=x_codes[:, s, j, g, :].bitcast(FP8X4),
                         lhsT_scale=x_planes[:, s, j, g, :],
-                        rhs=w_codes[:, slot, columns(half)].bitcast(FP8X4),
-                        rhs_scale=w_planes[plane_rows(slot) : P, slot // PLANES_PER_TILE, columns(half)],
+                        rhs=w_codes[:, slot, columns(block)].bitcast(FP8X4),
+                        rhs_scale=w_planes[plane_rows(slot) : P, slot // PLANES_PER_TILE, columns(block)],
                         start=(step == 0),
                         stop=(step == len(chain) - 1),
                     )
@@ -179,40 +185,40 @@ def tile_attention_two_encoder_pa_kernel(
         gate_chain = [(s, g, GROUPS * s + g) for s in range(SOURCES) for g in range(GROUPS)]
         gates = {}
 
-        def gate_round(half, tiles):
-            banks = product(gate_chain, half, tiles)
+        def gate_round(block, tiles):
+            banks = product(gate_chain, block, tiles)
             for j in tiles:
-                gates[j] = work.tile([P, N_PASS], F32, name="gate%d" % j, tag="gate", bufs=6)
+                gates[j] = work.tile([P, block[1]], F32, name="gate%d" % j, tag="gate", bufs=6)
                 nc.scalar.activation(out=gates[j][:], in_=banks[j][:], func=ACT.Sigmoid)
 
         mixes = {}
 
-        def blend(half, j):
-            from_sent = product(projection_chain(0), half, [j])[j]
-            kept = work.tile([P, N_PASS], F32)
+        def blend(block, j):
+            from_sent = product(projection_chain(0), block, [j])[j]
+            kept = work.tile([P, block[1]], F32)
             nc.vector.scalar_tensor_tensor(
                 out=kept[:], in0=gates[j][:], scalar=1.0, in1=from_sent[:], op0=ALU.subtract, op1=ALU.mult
             )
-            from_template = product(projection_chain(1), half, [j])[j]
-            taken = work.tile([P, N_PASS], F32)
+            from_template = product(projection_chain(1), block, [j])[j]
+            taken = work.tile([P, block[1]], F32)
             nc.vector.tensor_tensor(out=taken[:], in0=gates[j][:], in1=from_template[:], op=ALU.mult)
-            mixes[j] = work.tile([P, N_PASS], F32, name="mixed")
+            mixes[j] = work.tile([P, block[1]], F32, name="mixed")
             nc.gpsimd.tensor_tensor(out=mixes[j][:], in0=taken[:], in1=kept[:], op=ALU.subtract)
 
-        def finish(half, j):
-            from_output = product(projection_chain(2), half, [j])[j]
-            fusion = work.tile([P, N_PASS], F32)
+        def finish(block, j):
+            from_output = product(projection_chain(2), block, [j])[j]
+            fusion = work.tile([P, block[1]], F32)
             nc.vector.tensor_tensor(out=fusion[:], in0=mixes[j][:], in1=from_output[:], op=ALU.add)
-            result = work.tile([P, N_PASS], F32, bufs=8)
+            result = work.tile([P, block[1]], F32, bufs=8)
             nc.scalar.activation(out=result[:], in_=fusion[:], func=ACT.Tanh)
-            nc.sync.dma_start(out=out_rows[:, j, columns(half)], in_=result[:])
+            nc.sync.dma_start(out=out_rows[:, j, columns(block)], in_=result[:])
 
-        units = [(half, j) for half in range(HALVES) for j in range(TOKEN_TILES)]
-        gate_round(0, range(TOKEN_TILES))
-        for before, (half, j), after in zip([None] + units, units, units[1:] + [None]):
-            blend(half, j)
-            if after is not None and after[0] > 0:
+        units = [(block, j) for block in BLOCKS for j in range(TOKEN_TILES)]
+        gate_round(BLOCKS[0], range(TOKEN_TILES))
+        for before, (block, j), after in zip([None] + units, units, units[1:] + [None]):
+            blend(block, j)
+            if after is not None and after[0] != BLOCKS[0]:
                 gate_round(after[0], [after[1]])
             if before is not None:
                 finish(before[0], before[1])
-        finish(HALVES - 1, TOKEN_TILES - 1)
+        finish(units[-1][0], units[-1][1])

@@ -130,10 +130,10 @@ def tile_attention_two_encoder_pa_kernel(
             load_scales(scales, 0, GROUPS, GATE_SLOTS + GROUPS * s)
         for s, (words, scales) in enumerate(projections):
             load_codes(words, 0, GROUPS, GATE_SLOTS + GROUPS * s, HALVES[0])
-        for s in range(SOURCES):
-            load_codes(W_gate_words, GROUPS * s, GROUPS, GROUPS * s, HALVES[1])
-        for s, (words, scales) in enumerate(projections):
-            load_codes(words, 0, GROUPS, GATE_SLOTS + GROUPS * s, HALVES[1])
+        for block in BLOCKS[1:]:
+            load_codes(W_gate_words, 0, GATE_SLOTS, 0, block)
+            for s, (words, scales) in enumerate(projections):
+                load_codes(words, 0, GROUPS, GATE_SLOTS + GROUPS * s, block)
 
         def quantise(s, j):
             nc.vector.quantize_mx(

@@ -30,6 +30,7 @@ SLOTS = 2 * GATE_SLOTS
 PLANES_PER_TILE = 4
 QUADRANTS = 4
 LIVE_ROWS = 4
+FINISH_LAG = 3
 
 FLOPS = 2 * TOKENS * H * (SOURCES * H + SOURCES * H)
 
@@ -202,7 +203,7 @@ def tile_attention_two_encoder_pa_kernel(
             from_template = product(projection_chain(1), block, [j])[j]
             taken = work.tile([P, block[1]], F32)
             nc.vector.tensor_tensor(out=taken[:], in0=gates[j][:], in1=from_template[:], op=ALU.mult)
-            mixes[j] = work.tile([P, block[1]], F32, name="mixed")
+            mixes[j] = work.tile([P, block[1]], F32, name="mixed", bufs=FINISH_LAG + 3)
             nc.gpsimd.tensor_tensor(out=mixes[j][:], in0=taken[:], in1=kept[:], op=ALU.subtract)
 
         def finish(block, j):
@@ -215,10 +216,11 @@ def tile_attention_two_encoder_pa_kernel(
 
         units = [(block, j) for block in BLOCKS for j in range(TOKEN_TILES)]
         gate_round(BLOCKS[0], range(TOKEN_TILES))
-        for before, (block, j), after in zip([None] + units, units, units[1:] + [None]):
+        for turn, (block, j) in enumerate(units):
             blend(block, j)
-            if after is not None and after[0] != BLOCKS[0]:
-                gate_round(after[0], [after[1]])
-            if before is not None:
-                finish(before[0], before[1])
-        finish(units[-1][0], units[-1][1])
+            if turn + 1 < len(units) and units[turn + 1][0] != BLOCKS[0]:
+                gate_round(units[turn + 1][0], [units[turn + 1][1]])
+            if turn >= FINISH_LAG:
+                finish(units[turn - FINISH_LAG][0], units[turn - FINISH_LAG][1])
+        for block, j in units[len(units) - FINISH_LAG :]:
+            finish(block, j)

@@ -30,6 +30,7 @@ SLOTS = 2 * GATE_SLOTS
 PLANES_PER_TILE = 4
 QUADRANTS = 4
 LIVE_ROWS = 4
+PLANE_TILES = 4
 FINISH_LAG = 3
 
 FLOPS = 2 * TOKENS * H * (SOURCES * H + SOURCES * H)
@@ -75,7 +76,7 @@ def tile_attention_two_encoder_pa_kernel(
         x_codes = keep.tile([P, SOURCES, TOKEN_TILES, GROUPS, P], U32, align_bytes=64)
         x_planes = keep.tile([P, SOURCES, TOKEN_TILES, GROUPS, P], U8, align_bytes=64)
         w_codes = keep.tile([P, SLOTS, H], U32, align_bytes=64)
-        w_planes = keep.tile([P, SLOTS // PLANES_PER_TILE, H], U8, align_bytes=64)
+        w_planes = keep.tile([P, PLANE_TILES, H], U8, align_bytes=64)
         identity = keep.tile([P, P], F32)
         warm = keep.tile([P, 1], F32)
 
@@ -100,14 +101,20 @@ def tile_attention_two_encoder_pa_kernel(
                 .bitcast(I32),
             )
 
+        def plane_place(slot):
+            return slot if slot < GATE_SLOTS + 2 * GROUPS else slot + GROUPS
+
+        def plane_tile(slot):
+            return plane_place(slot) // PLANES_PER_TILE
+
         def plane_rows(slot):
-            return LIVE_ROWS * (slot % PLANES_PER_TILE)
+            return LIVE_ROWS * (plane_place(slot) % PLANES_PER_TILE)
 
         def load_scales(scales, first, count, slot):
             for quadrant in range(QUADRANTS):
                 top = 32 * quadrant + plane_rows(slot)
                 nc.sync.dma_start(
-                    out=w_planes[top : top + LIVE_ROWS * count, slot // PLANES_PER_TILE, :].bitcast(I32),
+                    out=w_planes[top : top + LIVE_ROWS * count, plane_tile(slot), :].bitcast(I32),
                     in_=scales[
                         first : first + count, LIVE_ROWS * quadrant : LIVE_ROWS * (quadrant + 1), :
                     ].bitcast(I32),
@@ -119,22 +126,31 @@ def tile_attention_two_encoder_pa_kernel(
             (W_output_words, W_output_scales),
         ]
 
-        load_source(0)
+        def load_projection_scales(s):
+            load_scales(projections[s][1], 0, GROUPS, GATE_SLOTS + GROUPS * s)
+
+        def load_projection_codes(s, part):
+            load_codes(projections[s][0], 0, GROUPS, GATE_SLOTS + GROUPS * s, part)
+
+        for s in range(SOURCES):
+            load_source(s)
         load_scales(W_gate_scales, 0, 4, 0)
-        load_source(1)
-        load_source(2)
-        load_codes(W_gate_words, 0, GROUPS, 0, HALVES[0])
-        load_scales(W_gate_scales, 4, 2, 4)
+        load_codes(W_gate_words, 0, 1, 0, HALVES[0])
+        load_codes(W_gate_words, 1, 1, 1, HALVES[0])
         load_codes(W_gate_words, 2, GROUPS, 2, HALVES[0])
+        load_scales(W_gate_scales, 4, 2, 4)
         load_codes(W_gate_words, 4, GROUPS, 4, HALVES[0])
-        for s, (words, scales) in enumerate(projections):
-            load_scales(scales, 0, GROUPS, GATE_SLOTS + GROUPS * s)
-        for s, (words, scales) in enumerate(projections):
-            load_codes(words, 0, GROUPS, GATE_SLOTS + GROUPS * s, HALVES[0])
+        load_projection_scales(0)
+        load_projection_codes(0, HALVES[0])
+        load_projection_codes(1, HALVES[0])
+        load_projection_scales(1)
+        load_projection_codes(2, HALVES[0])
         for block in BLOCKS[1:]:
             load_codes(W_gate_words, 0, GATE_SLOTS, 0, block)
-            for s, (words, scales) in enumerate(projections):
-                load_codes(words, 0, GROUPS, GATE_SLOTS + GROUPS * s, block)
+            if block == BLOCKS[1]:
+                load_projection_scales(2)
+            for s in range(SOURCES):
+                load_projection_codes(s, block)
 
         def quantise(s, j):
             nc.vector.quantize_mx(
@@ -174,7 +190,7 @@ def tile_attention_two_encoder_pa_kernel(
                         lhsT=x_codes[:, s, j, g, :].bitcast(FP8X4),
                         lhsT_scale=x_planes[:, s, j, g, :],
                         rhs=w_codes[:, slot, columns(block)].bitcast(FP8X4),
-                        rhs_scale=w_planes[plane_rows(slot) : P, slot // PLANES_PER_TILE, columns(block)],
+                        rhs_scale=w_planes[plane_rows(slot) : P, plane_tile(slot), columns(block)],
                         start=(step == 0),
                         stop=(step == len(chain) - 1),
                     )

@@ -31,7 +31,7 @@ PLANES_PER_TILE = 4
 QUADRANTS = 4
 LIVE_ROWS = 4
 PLANE_TILES = 4
-FINISH_LAG = 3
+FINISH_LAG = 4
 
 FLOPS = 2 * TOKENS * H * (SOURCES * H + SOURCES * H)
 
@@ -219,13 +219,13 @@ def tile_attention_two_encoder_pa_kernel(
             from_template = product(projection_chain(1), block, [j])[j]
             taken = work.tile([P, block[1]], F32)
             nc.vector.tensor_tensor(out=taken[:], in0=gates[j][:], in1=from_template[:], op=ALU.mult)
-            mixes[j] = work.tile([P, block[1]], F32, name="mixed", bufs=FINISH_LAG + 3)
-            nc.gpsimd.tensor_tensor(out=mixes[j][:], in0=taken[:], in1=kept[:], op=ALU.subtract)
+            mixes[block, j] = work.tile([P, block[1]], F32, name="mixed", bufs=FINISH_LAG + 3)
+            nc.gpsimd.tensor_tensor(out=mixes[block, j][:], in0=taken[:], in1=kept[:], op=ALU.subtract)
 
         def finish(block, j):
             from_output = product(projection_chain(2), block, [j])[j]
             fusion = work.tile([P, block[1]], F32)
-            nc.vector.tensor_tensor(out=fusion[:], in0=mixes[j][:], in1=from_output[:], op=ALU.add)
+            nc.vector.tensor_tensor(out=fusion[:], in0=mixes[block, j][:], in1=from_output[:], op=ALU.add)
             result = work.tile([P, block[1]], F32, bufs=8)
             nc.scalar.activation(out=result[:], in_=fusion[:], func=ACT.Tanh)
             nc.sync.dma_start(out=out_rows[:, j, columns(block)], in_=result[:])

@@ -144,13 +144,14 @@ def tile_attention_two_encoder_pa_kernel(
         load_projection_codes(0, HALVES[0])
         load_projection_codes(1, HALVES[0])
         load_projection_scales(1)
-        load_projection_codes(2, HALVES[0])
-        for block in BLOCKS[1:]:
+        for before, block in zip(BLOCKS, BLOCKS[1:]):
             load_codes(W_gate_words, 0, GATE_SLOTS, 0, block)
-            if block == BLOCKS[1]:
+            load_projection_codes(0, block)
+            load_projection_codes(1, block)
+            load_projection_codes(2, before)
+            if before == BLOCKS[0]:
                 load_projection_scales(2)
-            for s in range(SOURCES):
-                load_projection_codes(s, block)
+        load_projection_codes(2, BLOCKS[-1])
 
         def quantise(s, j):
             nc.vector.quantize_mx(

from contextlib import ExitStack

import concourse.mybir as mybir
from concourse.masks import make_identity

BF16 = mybir.dt.bfloat16
F32 = mybir.dt.float32
I32 = mybir.dt.int32
U32 = mybir.dt.uint32
U8 = mybir.dt.uint8
FP8X4 = mybir.dt.float8_e4m3fn_x4
ACT = mybir.ActivationFunctionType
ALU = mybir.AluOpType

P = 128
PACK = 4
K_PASS = P * PACK
PAIRS = K_PASS // 2
H = 1024
TOKENS = 512
TOKEN_TILES = TOKENS // P
SOURCES = 3
GROUPS = H // K_PASS
N_PASS = 512
HALVES = [(0, N_PASS), (N_PASS, N_PASS)]
BLOCKS = [(0, N_PASS), (N_PASS, N_PASS // 2), (N_PASS + N_PASS // 2, N_PASS // 2)]
TILES_PER_LOAD = 2
GATE_SLOTS = SOURCES * GROUPS
SLOTS = 2 * GATE_SLOTS
PLANES_PER_TILE = 4
QUADRANTS = 4
LIVE_ROWS = 4
PLANE_TILES = 4
FINISH_LAG = 4

FLOPS = 2 * TOKENS * H * (SOURCES * H + SOURCES * H)


def tile_attention_two_encoder_pa_kernel(
    tc,
    sent_ctx,
    template_ctx,
    output,
    W_gate_words,
    W_gate_scales,
    W_sent_words,
    W_sent_scales,
    W_template_words,
    W_template_scales,
    W_output_words,
    W_output_scales,
    out,
):
    nc = tc.nc
    sources = [sent_ctx, template_ctx, output]

    def by_partition(tensor):
        return tensor.rearrange("b t c -> (b t) c").rearrange("(p j) c -> p j c", j=TOKEN_TILES)

    out_rows = by_partition(out)

    with ExitStack() as stack:
        keep = stack.enter_context(tc.tile_pool(name="keep", bufs=1))
        work = stack.enter_context(tc.tile_pool(name="work", bufs=4))
        psum = stack.enter_context(tc.psum_pool(name="psum", bufs=8))
        stack.enter_context(tc.manual_schedule())

        x_rows = {}
        for s in range(SOURCES):
            for j in range(0, TOKEN_TILES, TILES_PER_LOAD):
                x_rows[s, j] = keep.tile([P, TILES_PER_LOAD, H], BF16, name="x_rows%d_%d" % (s, j))
        x_grouped = [
            keep.tile([P, TOKEN_TILES, GROUPS, P, PACK], BF16, name="x_grouped%d" % s, align_bytes=64)
            for s in range(SOURCES)
        ]
        x_codes = keep.tile([P, SOURCES, TOKEN_TILES, GROUPS, P], U32, align_bytes=64)
        x_planes = keep.tile([P, SOURCES, TOKEN_TILES, GROUPS, P], U8, align_bytes=64)
        w_codes = keep.tile([P, SLOTS, H], U32, align_bytes=64)
        w_planes = keep.tile([P, PLANE_TILES, H], U8, align_bytes=64)
        identity = keep.tile([P, P], F32)
        warm = keep.tile([P, 1], F32)

        nc.vector.memset(w_planes[:].bitcast(I32), 0)
        nc.vector.memset(warm[:], 0.0)
        nc.scalar.activation(out=warm[:], in_=warm[:], func=ACT.Sigmoid)
        make_identity(nc, identity[:])

        def load_source(s):
            for j in range(0, TOKEN_TILES, TILES_PER_LOAD):
                nc.sync.dma_start(out=x_rows[s, j][:], in_=by_partition(sources[s])[:, j : j + TILES_PER_LOAD, :])

        def columns(block):
            return slice(block[0], block[0] + block[1])

        def load_codes(words, first, count, slot, half):
            byte_columns = slice(half[0] * PACK, (half[0] + half[1]) * PACK)
            nc.sync.dma_start(
                out=w_codes[:, slot : slot + count, columns(half)].bitcast(I32),
                in_=words[first : first + count]
                .rearrange("g p n t -> p g (n t)")[:, :, byte_columns]
                .bitcast(I32),
            )

        def plane_place(slot):
            return slot if slot < GATE_SLOTS + 2 * GROUPS else slot + GROUPS

        def plane_tile(slot):
            return plane_place(slot) // PLANES_PER_TILE

        def plane_rows(slot):
            return LIVE_ROWS * (plane_place(slot) % PLANES_PER_TILE)

        def load_scales(scales, first, count, slot):
            for quadrant in range(QUADRANTS):
                top = 32 * quadrant + plane_rows(slot)
                nc.sync.dma_start(
                    out=w_planes[top : top + LIVE_ROWS * count, plane_tile(slot), :].bitcast(I32),
                    in_=scales[
                        first : first + count, LIVE_ROWS * quadrant : LIVE_ROWS * (quadrant + 1), :
                    ].bitcast(I32),
                )

        projections = [
            (W_sent_words, W_sent_scales),
            (W_template_words, W_template_scales),
            (W_output_words, W_output_scales),
        ]

        def load_projection_scales(s):
            load_scales(projections[s][1], 0, GROUPS, GATE_SLOTS + GROUPS * s)

        def load_projection_codes(s, part):
            load_codes(projections[s][0], 0, GROUPS, GATE_SLOTS + GROUPS * s, part)

        for s in range(SOURCES):
            load_source(s)
        load_scales(W_gate_scales, 0, 4, 0)
        load_codes(W_gate_words, 0, 1, 0, HALVES[0])
        load_codes(W_gate_words, 1, 1, 1, HALVES[0])
        load_codes(W_gate_words, 2, GROUPS, 2, HALVES[0])
        load_scales(W_gate_scales, 4, 2, 4)
        load_codes(W_gate_words, 4, GROUPS, 4, HALVES[0])
        load_projection_scales(0)
        load_projection_codes(0, HALVES[0])
        load_projection_codes(1, HALVES[0])
        load_projection_scales(1)
        for before, block in zip(BLOCKS, BLOCKS[1:]):
            load_codes(W_gate_words, 0, GATE_SLOTS, 0, block)
            load_projection_codes(0, block)
            load_projection_codes(1, block)
            load_projection_codes(2, before)
            if before == BLOCKS[0]:
                load_projection_scales(2)
        load_projection_codes(2, BLOCKS[-1])

        def quantise(s, j):
            nc.vector.quantize_mx(
                out=x_codes[:, s, j].rearrange("p g r -> p (g r)").bitcast(FP8X4),
                scales=x_planes[:, s, j].rearrange("p g r -> p (g r)"),
                in_=x_grouped[s][:, j].rearrange("p g r t -> p (g r t)"),
            )

        for s in range(SOURCES):
            for j in range(TOKEN_TILES):
                pairs = x_rows[s, j - j % TILES_PER_LOAD][:, j % TILES_PER_LOAD, :].bitcast(F32)
                flipped = psum.tile([P, GROUPS, 2, P], F32, tag="bank")
                for g in range(GROUPS):
                    for u in range(2):
                        nc.tensor.transpose(
                            flipped[:, g, u, :],
                            pairs[:, PAIRS * g + u : PAIRS * (g + 1) : 2],
                            identity[:],
                        )
                copy = nc.vector.tensor_copy if j == TOKEN_TILES - 1 else nc.scalar.copy
                copy(
                    out=x_grouped[s][:, j].bitcast(F32),
                    in_=flipped[:].rearrange("p g u r -> p g r u"),
                )
                if j > 0:
                    quantise(s, j - 1)
            quantise(s, TOKEN_TILES - 1)

        def product(chain, block, tiles):
            banks = {}
            for j in tiles:
                banks[j] = psum.tile([P, block[1]], F32, name="bank%d" % j, tag="bank")
            for step, (s, g, slot) in enumerate(chain):
                for j in tiles:
                    nc.tensor.matmul_mx(
                        out=banks[j][:],
                        lhsT=x_codes[:, s, j, g, :].bitcast(FP8X4),
                        lhsT_scale=x_planes[:, s, j, g, :],
                        rhs=w_codes[:, slot, columns(block)].bitcast(FP8X4),
                        rhs_scale=w_planes[plane_rows(slot) : P, plane_tile(slot), columns(block)],
                        start=(step == 0),
                        stop=(step == len(chain) - 1),
                    )
            return banks

        def projection_chain(s):
            return [(s, g, GATE_SLOTS + GROUPS * s + g) for g in range(GROUPS)]

        gate_chain = [(s, g, GROUPS * s + g) for s in range(SOURCES) for g in range(GROUPS)]
        gates = {}

        def gate_round(block, tiles):
            banks = product(gate_chain, block, tiles)
            for j in tiles:
                gates[j] = work.tile([P, block[1]], F32, name="gate%d" % j, tag="gate", bufs=6)
                nc.scalar.activation(out=gates[j][:], in_=banks[j][:], func=ACT.Sigmoid)

        mixes = {}

        def blend(block, j):
            from_sent = product(projection_chain(0), block, [j])[j]
            kept = work.tile([P, block[1]], F32)
            nc.vector.scalar_tensor_tensor(
                out=kept[:], in0=gates[j][:], scalar=1.0, in1=from_sent[:], op0=ALU.subtract, op1=ALU.mult
            )
            from_template = product(projection_chain(1), block, [j])[j]
            taken = work.tile([P, block[1]], F32)
            nc.vector.tensor_tensor(out=taken[:], in0=gates[j][:], in1=from_template[:], op=ALU.mult)
            mixes[block, j] = work.tile([P, block[1]], F32, name="mixed", bufs=FINISH_LAG + 3)
            nc.gpsimd.tensor_tensor(out=mixes[block, j][:], in0=taken[:], in1=kept[:], op=ALU.subtract)

        def finish(block, j):
            from_output = product(projection_chain(2), block, [j])[j]
            fusion = work.tile([P, block[1]], F32)
            nc.vector.tensor_tensor(out=fusion[:], in0=mixes[block, j][:], in1=from_output[:], op=ALU.add)
            result = work.tile([P, block[1]], F32, bufs=8)
            nc.scalar.activation(out=result[:], in_=fusion[:], func=ACT.Tanh)
            nc.sync.dma_start(out=out_rows[:, j, columns(block)], in_=result[:])

        units = [(block, j) for block in BLOCKS for j in range(TOKEN_TILES)]
        gate_round(BLOCKS[0], range(TOKEN_TILES))
        for turn, (block, j) in enumerate(units):
            blend(block, j)
            if turn + 1 < len(units) and units[turn + 1][0] != BLOCKS[0]:
                gate_round(units[turn + 1][0], [units[turn + 1][1]])
            if turn >= FINISH_LAG:
                finish(units[turn - FINISH_LAG][0], units[turn - FINISH_LAG][1])
        for block, j in units[len(units) - FINISH_LAG :]:
            finish(block, j)
